import numpy as np
import ml_dtypes


def mxq(x, axis, fmt="e4m3"):
    dtype, down = {"e4m3": (ml_dtypes.float8_e4m3fn, 7), "e5m2": (ml_dtypes.float8_e5m2, 14)}[fmt]
    v = np.moveaxis(np.asarray(x, np.float32).astype(ml_dtypes.bfloat16).astype(np.float64), axis, -1)
    blocks = v.reshape(v.shape[:-1] + (-1, 32))
    amax = np.abs(blocks).max(-1, keepdims=True)
    byte = np.maximum(np.where(amax > 0, np.frexp(amax)[1] - 1 + 127, 0) - down, 1)
    scale = np.exp2(byte - 127.0)
    codes = (blocks / scale).astype(np.float32).astype(dtype).astype(np.float64)
    return np.moveaxis((codes * scale).reshape(v.shape), -1, axis)


WIDE = False


def mx_kscale(k):
    if not WIDE:
        return np.ones(k)
    levels = np.array([10, -10, 5, -5, 0])
    if k % 512:
        return np.exp2(np.random.permutation(np.resize(levels, k // 32))).repeat(32)
    a = np.empty((k // 512, 16))
    for p in range(k // 512):
        a[p, :8] = np.random.permutation(np.resize(levels, 8))
        for g in range(8):
            far = levels[np.abs(levels - a[p, g]) >= 10]
            a[p, g + 8] = far[np.random.randint(len(far))]
    return np.exp2(a.ravel()).repeat(32)


BF16 = ml_dtypes.bfloat16


def bf(x):
    return np.asarray(x, np.float32).astype(BF16)


def f64(x):
    return np.asarray(x).astype(np.float64)


B, N, D, R = 1, 2048, 1024, 4
M = N // R


def merge(t, r):
    b, n, d = t.shape
    return t.reshape(b, n // r, r, d).mean(axis=2)


def setup_inputs():
    s, t = mx_kscale(D), mx_kscale(D)
    a = 2.0 / np.sqrt(D)
    return {"x": bf(np.random.standard_normal((B, N, D)) * s),
            "Wq": bf(np.random.standard_normal((D, D)) * a * t[:, None] / s),
            "bq": bf(np.random.standard_normal(D) * 0.5 * t),
            "Wk": bf(np.random.standard_normal((D, D)) * a / t[:, None] / s),
            "bk": bf(np.random.standard_normal(D) * 0.3 / t)}


def reference(x, Wq, bq, Wk, bk):
    xq = mxq(f64(x), 2, "e4m3")
    Q = (xq @ mxq(f64(Wq), 1, "e4m3").T) + f64(bq)
    K = (xq @ mxq(f64(Wk), 1, "e4m3").T) + f64(bk)
    K_m = merge(K, R)
    scores = (mxq(Q, 2, "e4m3") @ mxq(K_m, 2, "e4m3").transpose(0, 2, 1)) * (1.0 / np.sqrt(D))
    return scores + np.log(R)

@@ -1,0 +1,227 @@
+import math
+from contextlib import ExitStack
+
+import concourse.masks as masks
+import concourse.mybir as mybir
+
+BF16 = mybir.dt.bfloat16
+F32 = mybir.dt.float32
+U32 = mybir.dt.uint32
+U8 = mybir.dt.uint8
+FP8X4 = mybir.dt.float8_e4m3fn_x4
+ACT = mybir.ActivationFunctionType
+ALU = mybir.AluOpType
+
+P = 128
+PACK = 4
+K_PASS = P * PACK
+TOKENS = 2048
+FEATURES = 1024
+WINDOW = 4
+KEYS = TOKENS // WINDOW
+PASSES = FEATURES // K_PASS
+SLAB = 512
+SUB = SLAB // P
+W_SLABS = FEATURES // SLAB
+AHEAD = 3
+
+FLOPS = 2 * TOKENS * FEATURES * FEATURES * 2 + 2 * TOKENS * KEYS * FEATURES
+
+
+def tile_siglipsdpaattention_pa_kernel(tc, x, Wq, bq, Wk, bk, out):
+    nc = tc.nc
+    with ExitStack() as ctx:
+        keep = ctx.enter_context(tc.tile_pool(name="keep", bufs=1))
+        stage = ctx.enter_context(tc.tile_pool(name="stage", bufs=3))
+        result = ctx.enter_context(tc.tile_pool(name="result", bufs=6))
+        psum = ctx.enter_context(tc.psum_pool(name="psum", bufs=8))
+
+        def bank(name):
+            return psum.tile([P, SLAB], F32, name=name, tag="bank")
+
+        x_slabs = x.flatten_outer_dims().rearrange(
+            "(s p r) k -> r p s k", p=P, r=WINDOW
+        )
+        wq_slabs = Wq.rearrange("(G p s) k -> G p s k", p=P, s=SUB)
+        wk_slabs = Wk.rearrange("(G p s) k -> G p s k", p=P, s=SUB)
+        out_blocks = out.flatten_outer_dims().rearrange(
+            "(s p r) m -> r s p m", p=P, r=WINDOW
+        )
+
+        x_codes = keep.tile([P, WINDOW, PASSES, SLAB], U32, align_bytes=64)
+        x_scales = keep.tile([P, WINDOW, PASSES, SLAB], U8, align_bytes=64)
+        wq_codes = keep.tile([P, W_SLABS, PASSES, SLAB], U32, align_bytes=64)
+        wq_scales = keep.tile([P, W_SLABS, PASSES, SLAB], U8, align_bytes=64)
+        wk_codes = keep.tile([P, W_SLABS, PASSES, SLAB], U32, align_bytes=64)
+        wk_scales = keep.tile([P, W_SLABS, PASSES, SLAB], U8, align_bytes=64)
+        q_codes = keep.tile([P, PASSES, WINDOW, SLAB], U32, align_bytes=64)
+        q_scales = keep.tile([P, PASSES, WINDOW, SLAB], U8, align_bytes=64)
+        k_codes = keep.tile([P, PASSES, KEYS], U32, align_bytes=64)
+        k_scales = keep.tile([P, PASSES, KEYS], U8, align_bytes=64)
+
+        slabs = (
+            [(wk_slabs[0], wk_codes[:, 0], wk_scales[:, 0])]
+            + [(x_slabs[r], x_codes[:, r], x_scales[:, r]) for r in range(WINDOW)]
+            + [(wq_slabs[0], wq_codes[:, 0], wq_scales[:, 0])]
+            + [(wk_slabs[1], wk_codes[:, 1], wk_scales[:, 1])]
+            + [(wq_slabs[1], wq_codes[:, 1], wq_scales[:, 1])]
+        )
+        raws = []
+        for n, slab in enumerate(slabs):
+            raw = keep.tile([P, SUB, FEATURES], BF16, name="raw%d" % n)
+            for half in range(2):
+                pair = slice(2 * half, 2 * half + 2)
+                nc.sync.dma_start(out=raw[:, pair, :], in_=slab[0][:, pair, :])
+            raws.append(raw)
+
+        bq_bf = keep.tile([P, W_SLABS, SUB], BF16)
+        bk_bf = keep.tile([P, W_SLABS, SUB], BF16)
+        nc.scalar.dma_start(
+            out=bq_bf[:], in_=bq.rearrange("(G p s) -> p G s", p=P, s=SUB)
+        )
+        nc.scalar.dma_start(
+            out=bk_bf[:], in_=bk.rearrange("(G p s) -> p G s", p=P, s=SUB)
+        )
+        bq_f32 = keep.tile([P, W_SLABS, SUB], F32)
+        bk_f32 = keep.tile([P, W_SLABS, SUB], F32)
+
+        identity = keep.tile([P, P], F32)
+        masks.make_identity(nc, identity[:])
+
+        def prepare_slab(n):
+            raw = raws[n]
+            codes, scales = slabs[n][1], slabs[n][2]
+            grouped = stage.tile([P, PASSES * SLAB * PACK], BF16, align_bytes=64)
+            grouped_words = grouped[:].bitcast(F32).rearrange(
+                "p (g c u) -> p g c u", g=PASSES, u=2
+            )
+            for half in range(2):
+                for g in range(PASSES):
+                    turned = bank("turned")
+                    for s in range(2):
+                        words = raw[:, 2 * half + s, :].bitcast(F32)
+                        for u in range(2):
+                            nc.tensor.transpose(
+                                turned[:, (2 * s + u) * P : (2 * s + u + 1) * P],
+                                words[:, 2 * P * g + u : 2 * P * (g + 1) : 2],
+                                identity[:],
+                            )
+                    copy = nc.scalar.copy if g == 0 else nc.vector.tensor_copy
+                    copy(
+                        out=grouped_words[
+                            :, g, 2 * P * half : 2 * P * (half + 1), :
+                        ].rearrange("p (s c) u -> p s c u", s=2),
+                        in_=turned[:].rearrange("p (s u c) -> p s c u", s=2, u=2),
+                    )
+            for g in range(PASSES):
+                nc.vector.quantize_mx(
+                    out=codes[:, g, :].bitcast(FP8X4),
+                    scales=scales[:, g, :],
+                    in_=grouped[:, g * SLAB * PACK : (g + 1) * SLAB * PACK],
+                )
+
+        def project(acc, w_codes, w_scales, G, r, first, last):
+            for s in range(SUB):
+                cols = slice(s * P, (s + 1) * P)
+                for g in range(PASSES):
+                    nc.tensor.matmul_mx(
+                        out=acc[s][:],
+                        lhsT=w_codes[:, G, g, cols].bitcast(FP8X4),
+                        lhsT_scale=w_scales[:, G, g, cols],
+                        rhs=x_codes[:, r, g, :].bitcast(FP8X4),
+                        rhs_scale=x_scales[:, r, g, :],
+                        start=(first and g == 0),
+                        stop=(last and g == PASSES - 1),
+                    )
+
+        def finish(acc, scale, bias, codes, scales):
+            banks = stage.tile([P, SUB, SLAB], BF16)
+            for s in range(SUB):
+                nc.scalar.activation(
+                    out=banks[:, s, :],
+                    in_=acc[s][:],
+                    func=ACT.Identity,
+                    bias=bias[:, s : s + 1],
+                    scale=scale,
+                )
+            packed = stage.tile([P, SLAB, PACK], BF16, align_bytes=64)
+            nc.vector.tensor_copy(
+                out=packed[:].rearrange("p (c i) s -> p c s i", i=4),
+                in_=banks[:].rearrange("p s (c i) -> p c s i", i=4),
+            )
+            nc.vector.quantize_mx(
+                out=codes.bitcast(FP8X4),
+                scales=scales,
+                in_=packed[:].rearrange("p c s -> p (c s)"),
+            )
+
+        def query_unit(r, G):
+            acc = [bank("q_acc%d" % s) for s in range(SUB)]
+            project(acc, wq_codes, wq_scales, G, r, True, True)
+            finish(acc, 1.0, bq_f32[:, G, :], q_codes[:, G, r, :], q_scales[:, G, r, :])
+
+        def finish_keys(acc, G):
+            finish(
+                acc, 1.0 / WINDOW, bk_f32[:, G, :], k_codes[:, G, :], k_scales[:, G, :]
+            )
+
+        def score_unit(r):
+            acc = [bank("s_acc%d" % s) for s in range(SUB)]
+            for G in range(PASSES):
+                for s in range(SUB):
+                    cols = slice(s * P, (s + 1) * P)
+                    nc.tensor.matmul_mx(
+                        out=acc[s][:],
+                        lhsT=q_codes[:, G, r, cols].bitcast(FP8X4),
+                        lhsT_scale=q_scales[:, G, r, cols],
+                        rhs=k_codes[:, G, :].bitcast(FP8X4),
+                        rhs_scale=k_scales[:, G, :],
+                        start=(G == 0),
+                        stop=(G == PASSES - 1),
+                    )
+            for s in range(SUB):
+                logits = result.tile([P, KEYS], F32)
+                if s % 2 == 0:
+                    nc.vector.tensor_scalar(
+                        out=logits[:],
+                        in0=acc[s][:],
+                        scalar1=1.0 / math.sqrt(FEATURES),
+                        scalar2=math.log(WINDOW),
+                        op0=ALU.mult,
+                        op1=ALU.add,
+                    )
+                else:
+                    nc.scalar.activation(
+                        out=logits[:],
+                        in_=acc[s][:],
+                        func=ACT.Copy,
+                        bias=math.log(WINDOW),
+                        scale=1.0 / math.sqrt(FEATURES),
+                    )
+                nc.sync.dma_start(out=out_blocks[r, s], in_=logits[:])
+
+        for n in range(AHEAD):
+            prepare_slab(n)
+        nc.vector.tensor_copy(out=bq_f32[:], in_=bq_bf[:])
+        nc.vector.tensor_copy(out=bk_f32[:], in_=bk_bf[:])
+
+        k_acc = [bank("k_acc%d" % s) for s in range(SUB)]
+        for r in range(WINDOW):
+            project(k_acc, wk_codes, wk_scales, 0, r, r == 0, r == WINDOW - 1)
+            if r == WINDOW - 1:
+                finish_keys(k_acc, 0)
+            prepare_slab(AHEAD + r)
+
+        k_acc = [bank("k_acc%d" % s) for s in range(SUB)]
+        for r in range(WINDOW):
+            query_unit(r, 0)
+            if AHEAD + WINDOW + r < len(slabs):
+                prepare_slab(AHEAD + WINDOW + r)
+            project(k_acc, wk_codes, wk_scales, 1, r, r == 0, r == WINDOW - 1)
+        finish_keys(k_acc, 1)
+
+        for r in range(WINDOW):
+            query_unit(r, 1)
+            if r > 0:
+                score_unit(r - 1)
+        score_unit(WINDOW - 1)

@@ -22,8 +22,9 @@ KEYS = TOKENS // WINDOW
 PASSES = FEATURES // K_PASS
 SLAB = 512
 SUB = SLAB // P
+HALF = SLAB // 2
 W_SLABS = FEATURES // SLAB
-AHEAD = 3
+DIRECT = 4
 
 FLOPS = 2 * TOKENS * FEATURES * FEATURES * 2 + 2 * TOKENS * KEYS * FEATURES
 
@@ -31,13 +32,11 @@ FLOPS = 2 * TOKENS * FEATURES * FEATURES * 2 + 2 * TOKENS * KEYS * FEATURES
 def tile_siglipsdpaattention_pa_kernel(tc, x, Wq, bq, Wk, bk, out):
     nc = tc.nc
     with ExitStack() as ctx:
+        ctx.enter_context(tc.manual_schedule())
         keep = ctx.enter_context(tc.tile_pool(name="keep", bufs=1))
         stage = ctx.enter_context(tc.tile_pool(name="stage", bufs=3))
-        result = ctx.enter_context(tc.tile_pool(name="result", bufs=6))
-        psum = ctx.enter_context(tc.psum_pool(name="psum", bufs=8))
-
-        def bank(name):
-            return psum.tile([P, SLAB], F32, name=name, tag="bank")
+        result = ctx.enter_context(tc.tile_pool(name="result", bufs=12))
+        psum = ctx.enter_context(tc.psum_pool(name="psum", bufs=1))
 
         x_slabs = x.flatten_outer_dims().rearrange(
             "(s p r) k -> r p s k", p=P, r=WINDOW
@@ -59,19 +58,24 @@ def tile_siglipsdpaattention_pa_kernel(tc, x, Wq, bq, Wk, bk, out):
         k_codes = keep.tile([P, PASSES, KEYS], U32, align_bytes=64)
         k_scales = keep.tile([P, PASSES, KEYS], U8, align_bytes=64)
 
-        slabs = (
-            [(wk_slabs[0], wk_codes[:, 0], wk_scales[:, 0])]
-            + [(x_slabs[r], x_codes[:, r], x_scales[:, r]) for r in range(WINDOW)]
-            + [(wq_slabs[0], wq_codes[:, 0], wq_scales[:, 0])]
-            + [(wk_slabs[1], wk_codes[:, 1], wk_scales[:, 1])]
-            + [(wq_slabs[1], wq_codes[:, 1], wq_scales[:, 1])]
-        )
+        def wk(G, h):
+            return wk_slabs[G], wk_codes[:, G], wk_scales[:, G], h
+
+        def wq(G, h):
+            return wq_slabs[G], wq_codes[:, G], wq_scales[:, G], h
+
+        def xs(r, h):
+            return x_slabs[r], x_codes[:, r], x_scales[:, r], h
+
+        halves = [wk(0, 0), xs(0, 0), xs(0, 1), wk(0, 1)]
+        for r in range(1, WINDOW):
+            halves += [xs(r, 0), xs(r, 1)]
+        halves += [wk(1, 0), wk(1, 1), wq(0, 0), wq(0, 1), wq(1, 0), wq(1, 1)]
+
         raws = []
-        for n, slab in enumerate(slabs):
-            raw = keep.tile([P, SUB, FEATURES], BF16, name="raw%d" % n)
-            for half in range(2):
-                pair = slice(2 * half, 2 * half + 2)
-                nc.sync.dma_start(out=raw[:, pair, :], in_=slab[0][:, pair, :])
+        for n, (src, codes, scales, h) in enumerate(halves):
+            raw = keep.tile([P, 2, FEATURES], BF16, name="raw%d" % n)
+            nc.sync.dma_start(out=raw[:], in_=src[:, 2 * h : 2 * h + 2, :])
             raws.append(raw)
 
         bq_bf = keep.tile([P, W_SLABS, SUB], BF16)
@@ -88,40 +92,67 @@ def tile_siglipsdpaattention_pa_kernel(tc, x, Wq, bq, Wk, bk, out):
         identity = keep.tile([P, P], F32)
         masks.make_identity(nc, identity[:])
 
-        def prepare_slab(n):
-            raw = raws[n]
-            codes, scales = slabs[n][1], slabs[n][2]
-            grouped = stage.tile([P, PASSES * SLAB * PACK], BF16, align_bytes=64)
-            grouped_words = grouped[:].bitcast(F32).rearrange(
-                "p (g c u) -> p g c u", g=PASSES, u=2
+        def bank(i):
+            return psum.tile([P, SLAB], F32, name="bank%d" % i)
+
+        splits = {}
+        turned = {}
+        grouped = {}
+
+        def split(n):
+            t = stage.tile([P, 2, PASSES, 2, P], F32, name="split")
+            nc.vector.tensor_copy(
+                out=t[:].rearrange("p s g u i -> p (s g) u i"),
+                in_=raws[n][:].bitcast(F32).rearrange(
+                    "p s (g i u) -> p (s g) u i", g=PASSES, u=2
+                ),
             )
-            for half in range(2):
-                for g in range(PASSES):
-                    turned = bank("turned")
-                    for s in range(2):
-                        words = raw[:, 2 * half + s, :].bitcast(F32)
-                        for u in range(2):
-                            nc.tensor.transpose(
-                                turned[:, (2 * s + u) * P : (2 * s + u + 1) * P],
-                                words[:, 2 * P * g + u : 2 * P * (g + 1) : 2],
-                                identity[:],
-                            )
-                    copy = nc.scalar.copy if g == 0 else nc.vector.tensor_copy
-                    copy(
-                        out=grouped_words[
-                            :, g, 2 * P * half : 2 * P * (half + 1), :
-                        ].rearrange("p (s c) u -> p s c u", s=2),
-                        in_=turned[:].rearrange("p (s u c) -> p s c u", s=2, u=2),
-                    )
+            splits[n] = t
+
+        def turn(n, banks):
+            pair = []
             for g in range(PASSES):
-                nc.vector.quantize_mx(
-                    out=codes[:, g, :].bitcast(FP8X4),
-                    scales=scales[:, g, :],
-                    in_=grouped[:, g * SLAB * PACK : (g + 1) * SLAB * PACK],
+                t = bank(banks[g])
+                for s in range(2):
+                    words = raws[n][:, s, :].bitcast(F32)
+                    for u in range(2):
+                        if n < DIRECT:
+                            src = words[:, 2 * P * g + u : 2 * P * (g + 1) : 2]
+                        else:
+                            src = splits[n][:, s, g, u, :]
+                        nc.tensor.transpose(
+                            t[:, (2 * s + u) * P : (2 * s + u + 1) * P],
+                            src,
+                            identity[:],
+                        )
+                pair.append(t)
+            turned[n] = pair
+            grouped[n] = stage.tile(
+                [P, PASSES, HALF * PACK], BF16, name="grouped", align_bytes=64
+            )
+
+        def unload(n, engines):
+            for g in range(PASSES):
+                copy = nc.scalar.copy if engines[g] == "S" else nc.vector.tensor_copy
+                copy(
+                    out=grouped[n][:, g, :]
+                    .bitcast(F32)
+                    .rearrange("p (s c u) -> p s c u", s=2, u=2),
+                    in_=turned[n][g][:].rearrange("p (s u c) -> p s c u", s=2, u=2),
                 )
 
-        def project(acc, w_codes, w_scales, G, r, first, last):
-            for s in range(SUB):
+        def quant(n):
+            src, codes, scales, h = halves[n]
+            cols = slice(h * HALF, (h + 1) * HALF)
+            for g in range(PASSES):
+                nc.vector.quantize_mx(
+                    out=codes[:, g, cols].bitcast(FP8X4),
+                    scales=scales[:, g, cols],
+                    in_=grouped[n][:, g, :],
+                )
+
+        def project(acc, subs, w_codes, w_scales, G, r, first, last):
+            for s in subs:
                 cols = slice(s * P, (s + 1) * P)
                 for g in range(PASSES):
                     nc.tensor.matmul_mx(
@@ -134,42 +165,72 @@ def tile_siglipsdpaattention_pa_kernel(tc, x, Wq, bq, Wk, bk, out):
                         stop=(last and g == PASSES - 1),
                     )
 
-        def finish(acc, scale, bias, codes, scales):
-            banks = stage.tile([P, SUB, SLAB], BF16)
-            for s in range(SUB):
+        outs = {}
+
+        def empty(key, acc, subs, scale, bias):
+            if key not in outs:
+                outs[key] = stage.tile([P, SUB, SLAB], BF16, name="banks")
+            for s in subs:
                 nc.scalar.activation(
-                    out=banks[:, s, :],
+                    out=outs[key][:, s, :],
                     in_=acc[s][:],
                     func=ACT.Identity,
                     bias=bias[:, s : s + 1],
                     scale=scale,
                 )
-            packed = stage.tile([P, SLAB, PACK], BF16, align_bytes=64)
+
+        def pack(key):
+            packed = stage.tile([P, SLAB, PACK], BF16, name="packed", align_bytes=64)
             nc.vector.tensor_copy(
                 out=packed[:].rearrange("p (c i) s -> p c s i", i=4),
-                in_=banks[:].rearrange("p s (c i) -> p c s i", i=4),
+                in_=outs[key][:].rearrange("p s (c i) -> p c s i", i=4),
             )
+            outs[key] = packed
+
+        def code(key, codes, scales):
             nc.vector.quantize_mx(
                 out=codes.bitcast(FP8X4),
                 scales=scales,
-                in_=packed[:].rearrange("p c s -> p (c s)"),
+                in_=outs[key][:].rearrange("p c s -> p (c s)"),
             )
 
-        def query_unit(r, G):
-            acc = [bank("q_acc%d" % s) for s in range(SUB)]
-            project(acc, wq_codes, wq_scales, G, r, True, True)
-            finish(acc, 1.0, bq_f32[:, G, :], q_codes[:, G, r, :], q_scales[:, G, r, :])
+        k_acc = {}
 
-        def finish_keys(acc, G):
-            finish(
-                acc, 1.0 / WINDOW, bk_f32[:, G, :], k_codes[:, G, :], k_scales[:, G, :]
-            )
+        def keys(G, subs, banks, r):
+            if r == 0:
+                for s, b in zip(subs, banks):
+                    k_acc[G, s] = bank(b)
+            acc = [k_acc.get((G, s)) for s in range(SUB)]
+            project(acc, subs, wk_codes, wk_scales, G, r, r == 0, r == WINDOW - 1)
 
-        def score_unit(r):
-            acc = [bank("s_acc%d" % s) for s in range(SUB)]
-            for G in range(PASSES):
-                for s in range(SUB):
-                    cols = slice(s * P, (s + 1) * P)
+        def keys_empty(G, subs):
+            acc = [k_acc.get((G, s)) for s in range(SUB)]
+            empty(("k", G), acc, subs, 1.0 / WINDOW, bk_f32[:, G, :])
+
+        def keys_pack(G):
+            pack(("k", G))
+
+        def keys_code(G):
+            code(("k", G), k_codes[:, G, :], k_scales[:, G, :])
+
+        def query(r, G, banks):
+            acc = [bank(b) for b in banks]
+            project(acc, range(SUB), wq_codes, wq_scales, G, r, True, True)
+            empty(("q", G, r), acc, range(SUB), 1.0, bq_f32[:, G, :])
+
+        def query_pack(r, G):
+            pack(("q", G, r))
+
+        def query_code(r, G):
+            code(("q", G, r), q_codes[:, G, r, :], q_scales[:, G, r, :])
+
+        scores = {}
+
+        def score(r, banks):
+            acc = [bank(b) for b in banks]
+            for s in range(SUB):
+                cols = slice(s * P, (s + 1) * P)
+                for G in range(PASSES):
                     nc.tensor.matmul_mx(
                         out=acc[s][:],
                         lhsT=q_codes[:, G, r, cols].bitcast(FP8X4),
@@ -179,12 +240,15 @@ def tile_siglipsdpaattention_pa_kernel(tc, x, Wq, bq, Wk, bk, out):
                         start=(G == 0),
                         stop=(G == PASSES - 1),
                     )
+            scores[r] = acc
+
+        def deliver(r):
             for s in range(SUB):
                 logits = result.tile([P, KEYS], F32)
                 if s % 2 == 0:
                     nc.vector.tensor_scalar(
                         out=logits[:],
-                        in0=acc[s][:],
+                        in0=scores[r][s][:],
                         scalar1=1.0 / math.sqrt(FEATURES),
                         scalar2=math.log(WINDOW),
                         op0=ALU.mult,
@@ -193,35 +257,113 @@ def tile_siglipsdpaattention_pa_kernel(tc, x, Wq, bq, Wk, bk, out):
                 else:
                     nc.scalar.activation(
                         out=logits[:],
-                        in_=acc[s][:],
+                        in_=scores[r][s][:],
                         func=ACT.Copy,
                         bias=math.log(WINDOW),
                         scale=1.0 / math.sqrt(FEATURES),
                     )
                 nc.sync.dma_start(out=out_blocks[r, s], in_=logits[:])
 
-        for n in range(AHEAD):
-            prepare_slab(n)
+
+        ALL, LOW, HIGH = (0, 1, 2, 3), (0, 1), (2, 3)
+        KB = (0, 1, 2, 3)
+        T1, T2 = (4, 5), (6, 7)
+
+        def bring(n, banks, engines):
+            turn(n, banks)
+            unload(n, engines)
+
+        bring(0, T1, "SV")
+        quant(0)
+        bring(1, T2, "SV")
+        quant(1)
+        bring(2, T1, "SV")
+        quant(2)
+        split(4)
+        bring(3, T2, "SS")
+        keys(0, LOW, LOW, 0)
+        quant(3)
+        split(5)
+        bring(4, T1, "SS")
+        split(6)
+        bring(5, T2, "SS")
+        quant(4)
+        keys(0, HIGH, HIGH, 0)
+        split(7)
+        quant(5)
+        bring(6, T1, "SS")
+        bring(7, T2, "VS")
+        split(8)
+        keys(0, ALL, KB, 1)
+        quant(6)
+        split(9)
+        quant(7)
+        bring(8, T1, "SS")
+        bring(9, T2, "SV")
+        keys(0, ALL, KB, 2)
+        split(10)
+        quant(8)
+        split(11)
+        quant(9)
+        bring(10, T1, "SS")
+        bring(11, T2, "SV")
         nc.vector.tensor_copy(out=bq_f32[:], in_=bq_bf[:])
         nc.vector.tensor_copy(out=bk_f32[:], in_=bk_bf[:])
-
-        k_acc = [bank("k_acc%d" % s) for s in range(SUB)]
-        for r in range(WINDOW):
-            project(k_acc, wk_codes, wk_scales, 0, r, r == 0, r == WINDOW - 1)
-            if r == WINDOW - 1:
-                finish_keys(k_acc, 0)
-            prepare_slab(AHEAD + r)
-
-        k_acc = [bank("k_acc%d" % s) for s in range(SUB)]
-        for r in range(WINDOW):
-            query_unit(r, 0)
-            if AHEAD + WINDOW + r < len(slabs):
-                prepare_slab(AHEAD + WINDOW + r)
-            project(k_acc, wk_codes, wk_scales, 1, r, r == 0, r == WINDOW - 1)
-        finish_keys(k_acc, 1)
-
-        for r in range(WINDOW):
-            query_unit(r, 1)
-            if r > 0:
-                score_unit(r - 1)
-        score_unit(WINDOW - 1)
+        keys(0, ALL, KB, 3)
+        keys_empty(0, ALL)
+        split(12)
+        quant(10)
+        split(13)
+        quant(11)
+        bring(12, T1, "VV")
+        bring(13, T2, "SS")
+        keys(1, ALL, KB, 0)
+        quant(12)
+        keys_pack(0)
+        split(14)
+        quant(13)
+        keys_code(0)
+        keys(1, ALL, KB, 1)
+        split(15)
+        bring(14, T1, "SS")
+        bring(15, T2, "SS")
+        keys(1, ALL, KB, 2)
+        quant(14)
+        quant(15)
+        keys(1, ALL, KB, 3)
+        keys_empty(1, ALL)
+        X, Y = (4, 5, 6, 7), (0, 1, 2, 3)
+        query(0, 0, X)
+        keys_pack(1)
+        query(0, 1, Y)
+        keys_code(1)
+        query_pack(0, 0)
+        query(1, 0, X)
+        query_code(0, 0)
+        query_pack(0, 1)
+        query(1, 1, Y)
+        query_code(0, 1)
+        query_pack(1, 0)
+        score(0, X)
+        query_code(1, 0)
+        deliver(0)
+        query_pack(1, 1)
+        query(2, 0, Y)
+        query_code(1, 1)
+        query(2, 1, X)
+        query_pack(2, 0)
+        query_code(2, 0)
+        query(3, 0, Y)
+        query_pack(2, 1)
+        query_code(2, 1)
+        query(3, 1, X)
+        query_pack(3, 0)
+        query_code(3, 0)
+        score(1, Y)
+        query_pack(3, 1)
+        deliver(1)
+        query_code(3, 1)
+        score(2, X)
+        deliver(2)
+        score(3, Y)
+        deliver(3)

@@ -95,6 +95,14 @@ def tile_siglipsdpaattention_pa_kernel(tc, x, Wq, bq, Wk, bk, out):
         def bank(i):
             return psum.tile([P, SLAB], F32, name="bank%d" % i)
 
+        zeros = keep.tile([P, SLAB], BF16)
+        nc.vector.memset(zeros[:], 0.0)
+        idle = bank(7)
+        for i in range(5):
+            nc.tensor.matmul(
+                idle[:], lhsT=zeros[:, :P], rhs=zeros[:], start=True, stop=True
+            )
+
         splits = {}
         turned = {}
         grouped = {}

@@ -195,6 +195,33 @@ def tile_siglipsdpaattention_pa_kernel(tc, x, Wq, bq, Wk, bk, out):
             )
             outs[key] = packed
 
+        def query_halves(r, G, banks):
+            acc = [bank(b) for b in banks]
+            project(acc, range(SUB), wq_codes, wq_scales, G, r, True, True)
+            for h in range(2):
+                outs["q", G, r, h] = stage.tile([P, SUB, HALF], BF16, name="banks_half", bufs=2)
+            for s in range(SUB):
+                for h in range(2):
+                    nc.scalar.activation(
+                        out=outs["q", G, r, h][:, s, :],
+                        in_=acc[s][:, h * HALF : (h + 1) * HALF],
+                        func=ACT.Identity,
+                        bias=bq_f32[:, G, s : s + 1],
+                        scale=1.0,
+                    )
+
+        def half_pack(r, G, h):
+            packed = stage.tile([P, HALF, PACK], BF16, name="packed_half", bufs=2, align_bytes=64)
+            nc.vector.tensor_copy(
+                out=packed[:].rearrange("p (c i) s -> p c s i", i=4),
+                in_=outs["q", G, r, h][:].rearrange("p s (c i) -> p c s i", i=4),
+            )
+            outs["q", G, r, h] = packed
+
+        def half_code(r, G, h):
+            cols = slice(h * HALF, (h + 1) * HALF)
+            code(("q", G, r, h), q_codes[:, G, r, cols], q_scales[:, G, r, cols])
+
         def code(key, codes, scales):
             nc.vector.quantize_mx(
                 out=codes.bitcast(FP8X4),
@@ -234,13 +261,13 @@ def tile_siglipsdpaattention_pa_kernel(tc, x, Wq, bq, Wk, bk, out):
 
         scores = {}
 
-        def score(r, banks):
-            acc = [bank(b) for b in banks]
-            for s in range(SUB):
+        def score(r, banks, subs=range(SUB)):
+            for s, b in zip(subs, banks):
+                acc = bank(b)
                 cols = slice(s * P, (s + 1) * P)
                 for G in range(PASSES):
                     nc.tensor.matmul_mx(
-                        out=acc[s][:],
+                        out=acc[:],
                         lhsT=q_codes[:, G, r, cols].bitcast(FP8X4),
                         lhsT_scale=q_scales[:, G, r, cols],
                         rhs=k_codes[:, G, :].bitcast(FP8X4),
@@ -248,30 +275,51 @@ def tile_siglipsdpaattention_pa_kernel(tc, x, Wq, bq, Wk, bk, out):
                         start=(G == 0),
                         stop=(G == PASSES - 1),
                     )
-            scores[r] = acc
+                scores[r, s] = acc
 
-        def deliver(r):
-            for s in range(SUB):
+        def logit(engine, out_, in_):
+            if engine == "V":
+                nc.vector.tensor_scalar(
+                    out=out_,
+                    in0=in_,
+                    scalar1=1.0 / math.sqrt(FEATURES),
+                    scalar2=math.log(WINDOW),
+                    op0=ALU.mult,
+                    op1=ALU.add,
+                )
+            else:
+                nc.scalar.activation(
+                    out=out_,
+                    in_=in_,
+                    func=ACT.Copy,
+                    bias=math.log(WINDOW),
+                    scale=1.0 / math.sqrt(FEATURES),
+                )
+
+        def deliver(r, subs=range(SUB), engines="VSVS"):
+            for s, engine in zip(subs, engines):
                 logits = result.tile([P, KEYS], F32)
-                if s % 2 == 0:
-                    nc.vector.tensor_scalar(
-                        out=logits[:],
-                        in0=scores[r][s][:],
-                        scalar1=1.0 / math.sqrt(FEATURES),
-                        scalar2=math.log(WINDOW),
-                        op0=ALU.mult,
-                        op1=ALU.add,
-                    )
-                else:
-                    nc.scalar.activation(
-                        out=logits[:],
-                        in_=scores[r][s][:],
-                        func=ACT.Copy,
-                        bias=math.log(WINDOW),
-                        scale=1.0 / math.sqrt(FEATURES),
-                    )
+                logit(engine, logits[:], scores[r, s][:])
                 nc.sync.dma_start(out=out_blocks[r, s], in_=logits[:])
 
+        def last_score(r, s, banks, engines):
+            cols = slice(s * P, (s + 1) * P)
+            for h in range(2):
+                half = slice(h * HALF, (h + 1) * HALF)
+                acc = bank(banks[h])
+                for G in range(PASSES):
+                    nc.tensor.matmul_mx(
+                        out=acc[:, :HALF],
+                        lhsT=q_codes[:, G, r, cols].bitcast(FP8X4),
+                        lhsT_scale=q_scales[:, G, r, cols],
+                        rhs=k_codes[:, G, half].bitcast(FP8X4),
+                        rhs_scale=k_scales[:, G, half],
+                        start=(G == 0),
+                        stop=(G == PASSES - 1),
+                    )
+                logits = result.tile([P, HALF], F32, name="half_logits", bufs=2)
+                logit(engines[h], logits[:], acc[:, :HALF])
+                nc.sync.dma_start(out=out_blocks[r, s][:, half], in_=logits[:])
 
         ALL, LOW, HIGH = (0, 1, 2, 3), (0, 1), (2, 3)
         KB = (0, 1, 2, 3)
@@ -361,17 +409,20 @@ def tile_siglipsdpaattention_pa_kernel(tc, x, Wq, bq, Wk, bk, out):
         query(2, 1, X)
         query_pack(2, 0)
         query_code(2, 0)
-        query(3, 0, Y)
+        score(1, Y)
         query_pack(2, 1)
+        deliver(1)
         query_code(2, 1)
-        query(3, 1, X)
+        query(3, 0, X)
+        query_halves(3, 1, Y)
         query_pack(3, 0)
         query_code(3, 0)
-        score(1, Y)
-        query_pack(3, 1)
-        deliver(1)
-        query_code(3, 1)
         score(2, X)
-        deliver(2)
-        score(3, Y)
-        deliver(3)
+        half_pack(3, 1, 0)
+        half_code(3, 1, 0)
+        half_pack(3, 1, 1)
+        half_code(3, 1, 1)
+        deliver(2, range(4), "SSSV")
+        score(3, Y[:3], range(3))
+        deliver(3, range(3), "VSV")
+        last_score(3, 3, (X[0], X[1]), "SV")

import math
from contextlib import ExitStack

import concourse.masks as masks
import concourse.mybir as mybir

BF16 = mybir.dt.bfloat16
F32 = mybir.dt.float32
U32 = mybir.dt.uint32
U8 = mybir.dt.uint8
FP8X4 = mybir.dt.float8_e4m3fn_x4
ACT = mybir.ActivationFunctionType
ALU = mybir.AluOpType

P = 128
PACK = 4
K_PASS = P * PACK
TOKENS = 2048
FEATURES = 1024
WINDOW = 4
KEYS = TOKENS // WINDOW
PASSES = FEATURES // K_PASS
SLAB = 512
SUB = SLAB // P
HALF = SLAB // 2
W_SLABS = FEATURES // SLAB
DIRECT = 4

FLOPS = 2 * TOKENS * FEATURES * FEATURES * 2 + 2 * TOKENS * KEYS * FEATURES


def tile_siglipsdpaattention_pa_kernel(tc, x, Wq, bq, Wk, bk, out):
    nc = tc.nc
    with ExitStack() as ctx:
        ctx.enter_context(tc.manual_schedule())
        keep = ctx.enter_context(tc.tile_pool(name="keep", bufs=1))
        stage = ctx.enter_context(tc.tile_pool(name="stage", bufs=3))
        result = ctx.enter_context(tc.tile_pool(name="result", bufs=12))
        psum = ctx.enter_context(tc.psum_pool(name="psum", bufs=1))

        x_slabs = x.flatten_outer_dims().rearrange(
            "(s p r) k -> r p s k", p=P, r=WINDOW
        )
        wq_slabs = Wq.rearrange("(G p s) k -> G p s k", p=P, s=SUB)
        wk_slabs = Wk.rearrange("(G p s) k -> G p s k", p=P, s=SUB)
        out_blocks = out.flatten_outer_dims().rearrange(
            "(s p r) m -> r s p m", p=P, r=WINDOW
        )

        x_codes = keep.tile([P, WINDOW, PASSES, SLAB], U32, align_bytes=64)
        x_scales = keep.tile([P, WINDOW, PASSES, SLAB], U8, align_bytes=64)
        wq_codes = keep.tile([P, W_SLABS, PASSES, SLAB], U32, align_bytes=64)
        wq_scales = keep.tile([P, W_SLABS, PASSES, SLAB], U8, align_bytes=64)
        wk_codes = keep.tile([P, W_SLABS, PASSES, SLAB], U32, align_bytes=64)
        wk_scales = keep.tile([P, W_SLABS, PASSES, SLAB], U8, align_bytes=64)
        q_codes = keep.tile([P, PASSES, WINDOW, SLAB], U32, align_bytes=64)
        q_scales = keep.tile([P, PASSES, WINDOW, SLAB], U8, align_bytes=64)
        k_codes = keep.tile([P, PASSES, KEYS], U32, align_bytes=64)
        k_scales = keep.tile([P, PASSES, KEYS], U8, align_bytes=64)

        def wk(G, h):
            return wk_slabs[G], wk_codes[:, G], wk_scales[:, G], h

        def wq(G, h):
            return wq_slabs[G], wq_codes[:, G], wq_scales[:, G], h

        def xs(r, h):
            return x_slabs[r], x_codes[:, r], x_scales[:, r], h

        halves = [wk(0, 0), xs(0, 0), xs(0, 1), wk(0, 1)]
        for r in range(1, WINDOW):
            halves += [xs(r, 0), xs(r, 1)]
        halves += [wk(1, 0), wk(1, 1), wq(0, 0), wq(0, 1), wq(1, 0), wq(1, 1)]

        raws = []
        for n, (src, codes, scales, h) in enumerate(halves):
            raw = keep.tile([P, 2, FEATURES], BF16, name="raw%d" % n)
            nc.sync.dma_start(out=raw[:], in_=src[:, 2 * h : 2 * h + 2, :])
            raws.append(raw)

        bq_bf = keep.tile([P, W_SLABS, SUB], BF16)
        bk_bf = keep.tile([P, W_SLABS, SUB], BF16)
        nc.scalar.dma_start(
            out=bq_bf[:], in_=bq.rearrange("(G p s) -> p G s", p=P, s=SUB)
        )
        nc.scalar.dma_start(
            out=bk_bf[:], in_=bk.rearrange("(G p s) -> p G s", p=P, s=SUB)
        )
        bq_f32 = keep.tile([P, W_SLABS, SUB], F32)
        bk_f32 = keep.tile([P, W_SLABS, SUB], F32)

        identity = keep.tile([P, P], F32)
        masks.make_identity(nc, identity[:])

        def bank(i):
            return psum.tile([P, SLAB], F32, name="bank%d" % i)

        zeros = keep.tile([P, SLAB], BF16)
        nc.vector.memset(zeros[:], 0.0)
        idle = bank(7)
        for i in range(5):
            nc.tensor.matmul(
                idle[:], lhsT=zeros[:, :P], rhs=zeros[:], start=True, stop=True
            )

        splits = {}
        turned = {}
        grouped = {}

        def split(n):
            t = stage.tile([P, 2, PASSES, 2, P], F32, name="split")
            nc.vector.tensor_copy(
                out=t[:].rearrange("p s g u i -> p (s g) u i"),
                in_=raws[n][:].bitcast(F32).rearrange(
                    "p s (g i u) -> p (s g) u i", g=PASSES, u=2
                ),
            )
            splits[n] = t

        def turn(n, banks):
            pair = []
            for g in range(PASSES):
                t = bank(banks[g])
                for s in range(2):
                    words = raws[n][:, s, :].bitcast(F32)
                    for u in range(2):
                        if n < DIRECT:
                            src = words[:, 2 * P * g + u : 2 * P * (g + 1) : 2]
                        else:
                            src = splits[n][:, s, g, u, :]
                        nc.tensor.transpose(
                            t[:, (2 * s + u) * P : (2 * s + u + 1) * P],
                            src,
                            identity[:],
                        )
                pair.append(t)
            turned[n] = pair
            grouped[n] = stage.tile(
                [P, PASSES, HALF * PACK], BF16, name="grouped", align_bytes=64
            )

        def unload(n, engines):
            for g in range(PASSES):
                copy = nc.scalar.copy if engines[g] == "S" else nc.vector.tensor_copy
                copy(
                    out=grouped[n][:, g, :]
                    .bitcast(F32)
                    .rearrange("p (s c u) -> p s c u", s=2, u=2),
                    in_=turned[n][g][:].rearrange("p (s u c) -> p s c u", s=2, u=2),
                )

        def quant(n):
            src, codes, scales, h = halves[n]
            cols = slice(h * HALF, (h + 1) * HALF)
            for g in range(PASSES):
                nc.vector.quantize_mx(
                    out=codes[:, g, cols].bitcast(FP8X4),
                    scales=scales[:, g, cols],
                    in_=grouped[n][:, g, :],
                )

        def project(acc, subs, w_codes, w_scales, G, r, first, last):
            for s in subs:
                cols = slice(s * P, (s + 1) * P)
                for g in range(PASSES):
                    nc.tensor.matmul_mx(
                        out=acc[s][:],
                        lhsT=w_codes[:, G, g, cols].bitcast(FP8X4),
                        lhsT_scale=w_scales[:, G, g, cols],
                        rhs=x_codes[:, r, g, :].bitcast(FP8X4),
                        rhs_scale=x_scales[:, r, g, :],
                        start=(first and g == 0),
                        stop=(last and g == PASSES - 1),
                    )

        outs = {}

        def empty(key, acc, subs, scale, bias):
            if key not in outs:
                outs[key] = stage.tile([P, SUB, SLAB], BF16, name="banks")
            for s in subs:
                nc.scalar.activation(
                    out=outs[key][:, s, :],
                    in_=acc[s][:],
                    func=ACT.Identity,
                    bias=bias[:, s : s + 1],
                    scale=scale,
                )

        def pack(key):
            packed = stage.tile([P, SLAB, PACK], BF16, name="packed", align_bytes=64)
            nc.vector.tensor_copy(
                out=packed[:].rearrange("p (c i) s -> p c s i", i=4),
                in_=outs[key][:].rearrange("p s (c i) -> p c s i", i=4),
            )
            outs[key] = packed

        def query_halves(r, G, banks):
            acc = [bank(b) for b in banks]
            project(acc, range(SUB), wq_codes, wq_scales, G, r, True, True)
            for h in range(2):
                outs["q", G, r, h] = stage.tile([P, SUB, HALF], BF16, name="banks_half", bufs=2)
            for s in range(SUB):
                for h in range(2):
                    nc.scalar.activation(
                        out=outs["q", G, r, h][:, s, :],
                        in_=acc[s][:, h * HALF : (h + 1) * HALF],
                        func=ACT.Identity,
                        bias=bq_f32[:, G, s : s + 1],
                        scale=1.0,
                    )

        def half_pack(r, G, h):
            packed = stage.tile([P, HALF, PACK], BF16, name="packed_half", bufs=2, align_bytes=64)
            nc.vector.tensor_copy(
                out=packed[:].rearrange("p (c i) s -> p c s i", i=4),
                in_=outs["q", G, r, h][:].rearrange("p s (c i) -> p c s i", i=4),
            )
            outs["q", G, r, h] = packed

        def half_code(r, G, h):
            cols = slice(h * HALF, (h + 1) * HALF)
            code(("q", G, r, h), q_codes[:, G, r, cols], q_scales[:, G, r, cols])

        def code(key, codes, scales):
            nc.vector.quantize_mx(
                out=codes.bitcast(FP8X4),
                scales=scales,
                in_=outs[key][:].rearrange("p c s -> p (c s)"),
            )

        k_acc = {}

        def keys(G, subs, banks, r):
            if r == 0:
                for s, b in zip(subs, banks):
                    k_acc[G, s] = bank(b)
            acc = [k_acc.get((G, s)) for s in range(SUB)]
            project(acc, subs, wk_codes, wk_scales, G, r, r == 0, r == WINDOW - 1)

        def keys_empty(G, subs):
            acc = [k_acc.get((G, s)) for s in range(SUB)]
            empty(("k", G), acc, subs, 1.0 / WINDOW, bk_f32[:, G, :])

        def keys_pack(G):
            pack(("k", G))

        def keys_code(G):
            code(("k", G), k_codes[:, G, :], k_scales[:, G, :])

        def query(r, G, banks):
            acc = [bank(b) for b in banks]
            project(acc, range(SUB), wq_codes, wq_scales, G, r, True, True)
            empty(("q", G, r), acc, range(SUB), 1.0, bq_f32[:, G, :])

        def query_pack(r, G):
            pack(("q", G, r))

        def query_code(r, G):
            code(("q", G, r), q_codes[:, G, r, :], q_scales[:, G, r, :])

        scores = {}

        def score(r, banks, subs=range(SUB)):
            for s, b in zip(subs, banks):
                acc = bank(b)
                cols = slice(s * P, (s + 1) * P)
                for G in range(PASSES):
                    nc.tensor.matmul_mx(
                        out=acc[:],
                        lhsT=q_codes[:, G, r, cols].bitcast(FP8X4),
                        lhsT_scale=q_scales[:, G, r, cols],
                        rhs=k_codes[:, G, :].bitcast(FP8X4),
                        rhs_scale=k_scales[:, G, :],
                        start=(G == 0),
                        stop=(G == PASSES - 1),
                    )
                scores[r, s] = acc

        def logit(engine, out_, in_):
            if engine == "V":
                nc.vector.tensor_scalar(
                    out=out_,
                    in0=in_,
                    scalar1=1.0 / math.sqrt(FEATURES),
                    scalar2=math.log(WINDOW),
                    op0=ALU.mult,
                    op1=ALU.add,
                )
            else:
                nc.scalar.activation(
                    out=out_,
                    in_=in_,
                    func=ACT.Copy,
                    bias=math.log(WINDOW),
                    scale=1.0 / math.sqrt(FEATURES),
                )

        def deliver(r, subs=range(SUB), engines="VSVS"):
            for s, engine in zip(subs, engines):
                logits = result.tile([P, KEYS], F32)
                logit(engine, logits[:], scores[r, s][:])
                nc.sync.dma_start(out=out_blocks[r, s], in_=logits[:])

        def last_score(r, s, banks, engines):
            cols = slice(s * P, (s + 1) * P)
            for h in range(2):
                half = slice(h * HALF, (h + 1) * HALF)
                acc = bank(banks[h])
                for G in range(PASSES):
                    nc.tensor.matmul_mx(
                        out=acc[:, :HALF],
                        lhsT=q_codes[:, G, r, cols].bitcast(FP8X4),
                        lhsT_scale=q_scales[:, G, r, cols],
                        rhs=k_codes[:, G, half].bitcast(FP8X4),
                        rhs_scale=k_scales[:, G, half],
                        start=(G == 0),
                        stop=(G == PASSES - 1),
                    )
                logits = result.tile([P, HALF], F32, name="half_logits", bufs=2)
                logit(engines[h], logits[:], acc[:, :HALF])
                nc.sync.dma_start(out=out_blocks[r, s][:, half], in_=logits[:])

        ALL, LOW, HIGH = (0, 1, 2, 3), (0, 1), (2, 3)
        KB = (0, 1, 2, 3)
        T1, T2 = (4, 5), (6, 7)

        def bring(n, banks, engines):
            turn(n, banks)
            unload(n, engines)

        bring(0, T1, "SV")
        quant(0)
        bring(1, T2, "SV")
        quant(1)
        bring(2, T1, "SV")
        quant(2)
        split(4)
        bring(3, T2, "SS")
        keys(0, LOW, LOW, 0)
        quant(3)
        split(5)
        bring(4, T1, "SS")
        split(6)
        bring(5, T2, "SS")
        quant(4)
        keys(0, HIGH, HIGH, 0)
        split(7)
        quant(5)
        bring(6, T1, "SS")
        bring(7, T2, "VS")
        split(8)
        keys(0, ALL, KB, 1)
        quant(6)
        split(9)
        quant(7)
        bring(8, T1, "SS")
        bring(9, T2, "SV")
        keys(0, ALL, KB, 2)
        split(10)
        quant(8)
        split(11)
        quant(9)
        bring(10, T1, "SS")
        bring(11, T2, "SV")
        nc.vector.tensor_copy(out=bq_f32[:], in_=bq_bf[:])
        nc.vector.tensor_copy(out=bk_f32[:], in_=bk_bf[:])
        keys(0, ALL, KB, 3)
        keys_empty(0, ALL)
        split(12)
        quant(10)
        split(13)
        quant(11)
        bring(12, T1, "VV")
        bring(13, T2, "SS")
        keys(1, ALL, KB, 0)
        quant(12)
        keys_pack(0)
        split(14)
        quant(13)
        keys_code(0)
        keys(1, ALL, KB, 1)
        split(15)
        bring(14, T1, "SS")
        bring(15, T2, "SS")
        keys(1, ALL, KB, 2)
        quant(14)
        quant(15)
        keys(1, ALL, KB, 3)
        keys_empty(1, ALL)
        X, Y = (4, 5, 6, 7), (0, 1, 2, 3)
        query(0, 0, X)
        keys_pack(1)
        query(0, 1, Y)
        keys_code(1)
        query_pack(0, 0)
        query(1, 0, X)
        query_code(0, 0)
        query_pack(0, 1)
        query(1, 1, Y)
        query_code(0, 1)
        query_pack(1, 0)
        score(0, X)
        query_code(1, 0)
        deliver(0)
        query_pack(1, 1)
        query(2, 0, Y)
        query_code(1, 1)
        query(2, 1, X)
        query_pack(2, 0)
        query_code(2, 0)
        score(1, Y)
        query_pack(2, 1)
        deliver(1)
        query_code(2, 1)
        query(3, 0, X)
        query_halves(3, 1, Y)
        query_pack(3, 0)
        query_code(3, 0)
        score(2, X)
        half_pack(3, 1, 0)
        half_code(3, 1, 0)
        half_pack(3, 1, 1)
        half_code(3, 1, 1)
        deliver(2, range(4), "SSSV")
        score(3, Y[:3], range(3))
        deliver(3, range(3), "VSV")
        last_score(3, 3, (X[0], X[1]), "SV")
